import numpy as np
import ml_dtypes


def mxq(x, axis, fmt="e4m3"):
    dtype, down = {"e4m3": (ml_dtypes.float8_e4m3fn, 7), "e5m2": (ml_dtypes.float8_e5m2, 14)}[fmt]
    v = np.moveaxis(np.asarray(x, np.float32).astype(ml_dtypes.bfloat16).astype(np.float64), axis, -1)
    blocks = v.reshape(v.shape[:-1] + (-1, 32))
    amax = np.abs(blocks).max(-1, keepdims=True)
    byte = np.maximum(np.where(amax > 0, np.frexp(amax)[1] - 1 + 127, 0) - down, 1)
    scale = np.exp2(byte - 127.0)
    codes = (blocks / scale).astype(np.float32).astype(dtype).astype(np.float64)
    return np.moveaxis((codes * scale).reshape(v.shape), -1, axis)


WIDE = False


def mx_kscale(k):
    if not WIDE:
        return np.ones(k)
    levels = np.array([10, -10, 5, -5, 0])
    a = np.random.permutation(np.resize(levels, k // 512 * 4)).reshape(k // 512, 4)
    idx = np.arange(k)
    return np.exp2(a[idx // 512, idx % 128 // 32])


BF16 = ml_dtypes.bfloat16


def bf(x):
    return np.asarray(x, np.float32).astype(BF16)


def f64(x):
    return np.asarray(x).astype(np.float64)


B, L, LQ, DM, DH, W = 2, 8192, 1024, 512, 128, 512
C = L // W


def chunk_banks(x):
    z = np.zeros_like(x[:, :1])
    prev = np.concatenate((z, x[:, :-1]), axis=1)
    nxt = np.concatenate((x[:, 1:], z), axis=1)
    return np.stack((prev, x, nxt), axis=1).sum(axis=2)


def setup_inputs():
    s = mx_kscale(DM)
    return {"kv": bf(np.random.standard_normal((B, L, DM)) * s),
            "Wkv": bf(np.random.standard_normal((DM, 2 * DH)) * 2.0 / np.sqrt(DM * C) / s[:, None])}


def reference(kv, Wkv):
    kvp = mxq(f64(kv), 2, "e4m3") @ mxq(f64(Wkv), 0, "e4m3")
    k, v = kvp[..., :DH], kvp[..., DH:]
    return chunk_banks(k.reshape(B, C, W, DH)), v

@@ -1,0 +1,204 @@
+from contextlib import ExitStack
+
+import concourse.mybir as mybir
+from concourse.masks import make_identity
+
+F32 = mybir.dt.float32
+BF16 = mybir.dt.bfloat16
+U32 = mybir.dt.uint32
+U8 = mybir.dt.uint8
+FP8X4 = mybir.dt.float8_e4m3fn_x4
+ADD = mybir.AluOpType.add
+
+P = 128
+PACK = 4
+BATCH, LENGTH, D_MODEL, D_HEAD, CHUNK = 2, 8192, 512, 128, 512
+CHUNKS_PER_BATCH = LENGTH // CHUNK
+N_CHUNKS = BATCH * CHUNKS_PER_BATCH
+TILES = CHUNK // P
+BANK = 512
+WORDS = D_MODEL // 2
+
+ROUND = 2
+N_ROUNDS = N_CHUNKS // ROUND
+ROUNDS_PER_BATCH = CHUNKS_PER_BATCH // ROUND
+KV_BUFS = 16
+
+FLOPS = 2 * BATCH * LENGTH * D_MODEL * 2 * D_HEAD
+
+
+def tile_localxlattention_pa_t_kernel(tc, kv, Wkv, k_ext, v):
+    nc = tc.nc
+    with ExitStack() as ctx:
+        ctx.enter_context(tc.manual_schedule())
+        const = ctx.enter_context(tc.tile_pool(name="const", bufs=1))
+        kv_pool = ctx.enter_context(tc.tile_pool(name="kv", bufs=KV_BUFS))
+        mx_pool = ctx.enter_context(tc.tile_pool(name="mx", bufs=2 * ROUND))
+        v_pool = ctx.enter_context(tc.tile_pool(name="v", bufs=N_CHUNKS))
+        k_pool = ctx.enter_context(tc.tile_pool(name="k", bufs=BATCH))
+        turn_psum = ctx.enter_context(tc.psum_pool(name="turn", bufs=2 * ROUND))
+        v_psum = ctx.enter_context(tc.psum_pool(name="vp", bufs=2))
+        k_psum = ctx.enter_context(tc.psum_pool(name="kp", bufs=2))
+
+        kv_tiles = {}
+        quantised = {}
+        v_tiles = {}
+        k_sums = {}
+
+        def load(g):
+            b, c = divmod(g, CHUNKS_PER_BATCH)
+            x = kv_pool.tile([P, TILES * D_MODEL], BF16, name="x")
+            rows = kv[b, c * CHUNK : (c + 1) * CHUNK, :]
+            nc.sync.dma_start(out=x[:], in_=rows.rearrange("(p t) d -> p (t d)", t=TILES))
+            kv_tiles[g] = x
+
+        def transpose_and_regroup(g):
+            words = kv_tiles[g][:].bitcast(F32)
+            grouped = mx_pool.tile([P, CHUNK * PACK], BF16, name="grouped", align_bytes=64)
+            grouped_words = grouped[:].bitcast(F32).rearrange("q (n u) -> q n u", u=2)
+            for half in range(TILES // 2):
+                turned = turn_psum.tile([P, BANK], F32, name="turned")
+                by_half = turned[:].rearrange("q (u n) -> q u n", u=2)
+                for i in range(2):
+                    t = 2 * half + i
+                    for u in range(2):
+                        first = t * WORDS + u * P
+                        nc.tensor.transpose(
+                            by_half[:, u, i * P : (i + 1) * P], words[:, first : first + P], ident[:]
+                        )
+                nc.scalar.copy(
+                    out=grouped_words[:, 2 * half * P : 2 * (half + 1) * P, :],
+                    in_=by_half.rearrange("q u n -> q n u"),
+                )
+            return grouped
+
+        def quantise(g, grouped):
+            codes = mx_pool.tile([P, CHUNK], U32, name="codes", align_bytes=64)
+            scales = mx_pool.tile([P, CHUNK], U8, name="scales", align_bytes=64)
+            nc.vector.quantize_mx(out=codes[:].bitcast(FP8X4), scales=scales[:], in_=grouped[:])
+            quantised[g] = (codes, scales)
+
+        def multiply(g):
+            b, c = divmod(g, CHUNKS_PER_BATCH)
+            codes, scales = quantised[g]
+            start = c in (0, 1, CHUNKS_PER_BATCH - 1)
+            stop = c in (0, CHUNKS_PER_BATCH - 2, CHUNKS_PER_BATCH - 1)
+            if start:
+                k_sums[b]["acc"] = k_psum.tile([P, BANK], F32, name="k_acc")
+            nc.tensor.matmul_mx(
+                out=k_sums[b]["acc"][:],
+                lhsT=w_codes[:, 0:D_HEAD].bitcast(FP8X4),
+                lhsT_scale=w_scales[:, 0:D_HEAD],
+                rhs=codes[:].bitcast(FP8X4),
+                rhs_scale=scales[:],
+                start=start,
+                stop=stop,
+            )
+            v_acc = v_psum.tile([P, TILES, D_HEAD], F32, name="v_acc")
+            for t in range(TILES):
+                nc.tensor.matmul_mx(
+                    out=v_acc[:, t, :],
+                    lhsT=codes[:, t * P : (t + 1) * P].bitcast(FP8X4),
+                    lhsT_scale=scales[:, t * P : (t + 1) * P],
+                    rhs=w_codes[:, D_HEAD : 2 * D_HEAD].bitcast(FP8X4),
+                    rhs_scale=w_scales[:, D_HEAD : 2 * D_HEAD],
+                    start=True,
+                    stop=True,
+                )
+            return k_sums[b]["acc"], v_acc
+
+        def empty_banks(g, k_acc, v_acc):
+            b, c = divmod(g, CHUNKS_PER_BATCH)
+            v_sb = v_pool.tile([P, TILES, D_HEAD], F32, name="v_sb")
+            nc.vector.tensor_copy(out=v_sb[:], in_=v_acc[:])
+            v_tiles[g] = v_sb
+            k = k_sums[b]
+            if c == 0:
+                nc.scalar.copy(out=k["first"][:], in_=k_acc[:])
+            if c == CHUNKS_PER_BATCH - 2:
+                nc.scalar.copy(out=k["middle"][:], in_=k_acc[:])
+                nc.vector.tensor_tensor(
+                    out=k["banksT"][:, 0, :], in0=k["middle"][:], in1=k["first"][:], op=ADD
+                )
+            if c == CHUNKS_PER_BATCH - 1:
+                nc.vector.tensor_tensor(
+                    out=k["banksT"][:, 2, :], in0=k_acc[:], in1=k["middle"][:], op=ADD
+                )
+                nc.vector.tensor_tensor(
+                    out=k["banksT"][:, 1, :], in0=k_acc[:], in1=k["banksT"][:, 0, :], op=ADD
+                )
+
+        def turn_k_back(b):
+            k = k_sums[b]
+            for j in range(3):
+                turned = turn_psum.tile([P, BANK], F32, name="turned")
+                for t in range(TILES):
+                    nc.tensor.transpose(
+                        turned[:, t * D_HEAD : (t + 1) * D_HEAD],
+                        k["banksT"][:, j, t * P : (t + 1) * P],
+                        ident[:],
+                    )
+                if j % 2 == 0:
+                    nc.vector.tensor_copy(out=k["banks"][:, j, :], in_=turned[:])
+                else:
+                    nc.scalar.copy(out=k["banks"][:, j, :], in_=turned[:])
+
+        for g in range(KV_BUFS):
+            load(g)
+
+        ident = const.tile([P, P], F32, name="ident")
+        make_identity(nc, ident[:])
+
+        w_rows = const.tile([P, PACK, 2 * D_HEAD], BF16, name="w_rows")
+        nc.scalar.dma_start(
+            out=w_rows[:].rearrange("q (u e) n -> q u (e n)", u=2),
+            in_=Wkv.rearrange("(u q e) n -> q u (e n)", u=2, e=2),
+        )
+        w_grouped = const.tile([P, 2 * D_HEAD, PACK], BF16, name="w_grouped", align_bytes=64)
+        nc.vector.tensor_copy(out=w_grouped[:], in_=w_rows[:].rearrange("q j n -> q n j"))
+        w_codes = const.tile([P, 2 * D_HEAD], U32, name="w_codes", align_bytes=64)
+        w_scales = const.tile([P, 2 * D_HEAD], U8, name="w_scales", align_bytes=64)
+        nc.vector.quantize_mx(
+            out=w_codes[:].bitcast(FP8X4),
+            scales=w_scales[:],
+            in_=w_grouped[:].rearrange("q n j -> q (n j)"),
+        )
+
+        for b in range(BATCH):
+            k_sums[b] = {
+                "first": k_pool.tile([P, BANK], F32, name="k_first"),
+                "middle": k_pool.tile([P, BANK], F32, name="k_middle"),
+                "banksT": k_pool.tile([P, 3, BANK], F32, name="k_banksT"),
+                "banks": k_pool.tile([P, 3, BANK], F32, name="k_banks"),
+            }
+
+        for r in range(N_ROUNDS + 2):
+            if r >= 2 and (r - 1) % ROUNDS_PER_BATCH == 0:
+                turn_k_back((r - 2) // ROUNDS_PER_BATCH)
+            grouped_tiles = {}
+            products = {}
+            if r < N_ROUNDS:
+                for g in range(r * ROUND, (r + 1) * ROUND):
+                    grouped_tiles[g] = transpose_and_regroup(g)
+                    if g + KV_BUFS < N_CHUNKS:
+                        load(g + KV_BUFS)
+            if 1 <= r <= N_ROUNDS:
+                for g in range((r - 1) * ROUND, r * ROUND):
+                    products[g] = multiply(g)
+            for i in range(ROUND):
+                if r < N_ROUNDS:
+                    quantise(r * ROUND + i, grouped_tiles[r * ROUND + i])
+                if 1 <= r <= N_ROUNDS:
+                    empty_banks((r - 1) * ROUND + i, *products[(r - 1) * ROUND + i])
+
+        for b in range(BATCH):
+            for c in range(CHUNKS_PER_BATCH):
+                rows = v[b, c * CHUNK : (c + 1) * CHUNK, :]
+                nc.sync.dma_start(
+                    out=rows.rearrange("(p t) d -> p t d", t=TILES),
+                    in_=v_tiles[b * CHUNKS_PER_BATCH + c][:],
+                )
+            nc.sync.dma_start(
+                out=k_ext[b].rearrange("j (p t) d -> p j (t d)", t=TILES),
+                in_=k_sums[b]["banks"][:],
+            )

@@ -13,16 +13,16 @@ ADD = mybir.AluOpType.add
 P = 128
 PACK = 4
 BATCH, LENGTH, D_MODEL, D_HEAD, CHUNK = 2, 8192, 512, 128, 512
-CHUNKS_PER_BATCH = LENGTH // CHUNK
-N_CHUNKS = BATCH * CHUNKS_PER_BATCH
-TILES = CHUNK // P
+N_STEPS = LENGTH // CHUNK
+ROWS = BATCH * CHUNK
+TILES = ROWS // P
 BANK = 512
+HALVES = ROWS // BANK
+TILES_PER_HALF = TILES // HALVES
 WORDS = D_MODEL // 2
-
-ROUND = 2
-N_ROUNDS = N_CHUNKS // ROUND
-ROUNDS_PER_BATCH = CHUNKS_PER_BATCH // ROUND
-KV_BUFS = 16
+K_BANKS = 3
+FIRST, LAST = 0, N_STEPS - 1
+KV_BUFS = N_STEPS // 2
 
 FLOPS = 2 * BATCH * LENGTH * D_MODEL * 2 * D_HEAD
 
@@ -33,172 +33,176 @@ def tile_localxlattention_pa_t_kernel(tc, kv, Wkv, k_ext, v):
         ctx.enter_context(tc.manual_schedule())
         const = ctx.enter_context(tc.tile_pool(name="const", bufs=1))
         kv_pool = ctx.enter_context(tc.tile_pool(name="kv", bufs=KV_BUFS))
-        mx_pool = ctx.enter_context(tc.tile_pool(name="mx", bufs=2 * ROUND))
-        v_pool = ctx.enter_context(tc.tile_pool(name="v", bufs=N_CHUNKS))
-        k_pool = ctx.enter_context(tc.tile_pool(name="k", bufs=BATCH))
-        turn_psum = ctx.enter_context(tc.psum_pool(name="turn", bufs=2 * ROUND))
-        v_psum = ctx.enter_context(tc.psum_pool(name="vp", bufs=2))
-        k_psum = ctx.enter_context(tc.psum_pool(name="kp", bufs=2))
+        mx_pool = ctx.enter_context(tc.tile_pool(name="mx", bufs=2))
+        v_pool = ctx.enter_context(tc.tile_pool(name="v", bufs=N_STEPS))
+        turn_psum = ctx.enter_context(tc.psum_pool(name="turn", bufs=4))
+        v_psum = ctx.enter_context(tc.psum_pool(name="vp", bufs=HALVES))
+        k_psum = ctx.enter_context(tc.psum_pool(name="kp", bufs=HALVES))
 
         kv_tiles = {}
         quantised = {}
         v_tiles = {}
-        k_sums = {}
+        k_open = {}
 
-        def load(g):
-            b, c = divmod(g, CHUNKS_PER_BATCH)
+        def load(c):
             x = kv_pool.tile([P, TILES * D_MODEL], BF16, name="x")
-            rows = kv[b, c * CHUNK : (c + 1) * CHUNK, :]
-            nc.sync.dma_start(out=x[:], in_=rows.rearrange("(p t) d -> p (t d)", t=TILES))
-            kv_tiles[g] = x
+            for b in range(BATCH):
+                rows = kv[b, c * CHUNK : (c + 1) * CHUNK, :]
+                nc.sync.dma_start(
+                    out=x[b:P:BATCH, :], in_=rows.rearrange("(q t) d -> q (t d)", t=TILES)
+                )
+            kv_tiles[c] = x
 
-        def transpose_and_regroup(g):
-            words = kv_tiles[g][:].bitcast(F32)
-            grouped = mx_pool.tile([P, CHUNK * PACK], BF16, name="grouped", align_bytes=64)
-            grouped_words = grouped[:].bitcast(F32).rearrange("q (n u) -> q n u", u=2)
-            for half in range(TILES // 2):
+        def transpose_and_regroup(c):
+            words = kv_tiles[c][:].bitcast(F32)
+            grouped = mx_pool.tile([P, ROWS * PACK], BF16, name="grouped", align_bytes=64)
+            grouped_words = grouped[:].bitcast(F32).rearrange("w (n u) -> w n u", u=2)
+            for pair in range(TILES // 2):
                 turned = turn_psum.tile([P, BANK], F32, name="turned")
-                by_half = turned[:].rearrange("q (u n) -> q u n", u=2)
+                by_u = turned[:].rearrange("w (u n) -> w u n", u=2)
                 for i in range(2):
-                    t = 2 * half + i
+                    t = 2 * pair + i
                     for u in range(2):
                         first = t * WORDS + u * P
                         nc.tensor.transpose(
-                            by_half[:, u, i * P : (i + 1) * P], words[:, first : first + P], ident[:]
+                            by_u[:, u, i * P : (i + 1) * P], words[:, first : first + P], ident[:]
                         )
                 nc.scalar.copy(
-                    out=grouped_words[:, 2 * half * P : 2 * (half + 1) * P, :],
-                    in_=by_half.rearrange("q u n -> q n u"),
+                    out=grouped_words[:, 2 * pair * P : 2 * (pair + 1) * P, :],
+                    in_=by_u.rearrange("w u n -> w n u"),
                 )
+            codes = mx_pool.tile([P, ROWS], U32, name="codes", align_bytes=64)
+            scales = mx_pool.tile([P, ROWS], U8, name="scales", align_bytes=64)
+            quantised[c] = (codes, scales)
             return grouped
 
-        def quantise(g, grouped):
-            codes = mx_pool.tile([P, CHUNK], U32, name="codes", align_bytes=64)
-            scales = mx_pool.tile([P, CHUNK], U8, name="scales", align_bytes=64)
-            nc.vector.quantize_mx(out=codes[:].bitcast(FP8X4), scales=scales[:], in_=grouped[:])
-            quantised[g] = (codes, scales)
+        def quantise(c, h, grouped):
+            codes, scales = quantised[c]
+            cols = slice(h * BANK, (h + 1) * BANK)
+            nc.vector.quantize_mx(
+                out=codes[:, cols].bitcast(FP8X4),
+                scales=scales[:, cols],
+                in_=grouped[:, h * BANK * PACK : (h + 1) * BANK * PACK],
+            )
 
-        def multiply(g):
-            b, c = divmod(g, CHUNKS_PER_BATCH)
-            codes, scales = quantised[g]
-            start = c in (0, 1, CHUNKS_PER_BATCH - 1)
-            stop = c in (0, CHUNKS_PER_BATCH - 2, CHUNKS_PER_BATCH - 1)
+        def multiply(c, h):
+            codes, scales = quantised[c]
+            cols = slice(h * BANK, (h + 1) * BANK)
+            start = c in (FIRST, FIRST + 1, LAST)
+            stop = c in (FIRST, LAST - 1, LAST)
             if start:
-                k_sums[b]["acc"] = k_psum.tile([P, BANK], F32, name="k_acc")
+                k_open[h] = k_psum.tile([P, BANK], F32, name="k_acc")
             nc.tensor.matmul_mx(
-                out=k_sums[b]["acc"][:],
+                out=k_open[h][:],
                 lhsT=w_codes[:, 0:D_HEAD].bitcast(FP8X4),
                 lhsT_scale=w_scales[:, 0:D_HEAD],
-                rhs=codes[:].bitcast(FP8X4),
-                rhs_scale=scales[:],
+                rhs=codes[:, cols].bitcast(FP8X4),
+                rhs_scale=scales[:, cols],
                 start=start,
                 stop=stop,
             )
-            v_acc = v_psum.tile([P, TILES, D_HEAD], F32, name="v_acc")
-            for t in range(TILES):
+            v_acc = v_psum.tile([P, TILES_PER_HALF, D_HEAD], F32, name="v_acc")
+            for i in range(TILES_PER_HALF):
+                tile_cols = slice(h * BANK + i * P, h * BANK + (i + 1) * P)
                 nc.tensor.matmul_mx(
-                    out=v_acc[:, t, :],
-                    lhsT=codes[:, t * P : (t + 1) * P].bitcast(FP8X4),
-                    lhsT_scale=scales[:, t * P : (t + 1) * P],
+                    out=v_acc[:, i, :],
+                    lhsT=codes[:, tile_cols].bitcast(FP8X4),
+                    lhsT_scale=scales[:, tile_cols],
                     rhs=w_codes[:, D_HEAD : 2 * D_HEAD].bitcast(FP8X4),
                     rhs_scale=w_scales[:, D_HEAD : 2 * D_HEAD],
                     start=True,
                     stop=True,
                 )
-            return k_sums[b]["acc"], v_acc
+            return k_open[h], v_acc
 
-        def empty_banks(g, k_acc, v_acc):
-            b, c = divmod(g, CHUNKS_PER_BATCH)
-            v_sb = v_pool.tile([P, TILES, D_HEAD], F32, name="v_sb")
-            nc.vector.tensor_copy(out=v_sb[:], in_=v_acc[:])
-            v_tiles[g] = v_sb
-            k = k_sums[b]
-            if c == 0:
-                nc.scalar.copy(out=k["first"][:], in_=k_acc[:])
-            if c == CHUNKS_PER_BATCH - 2:
-                nc.scalar.copy(out=k["middle"][:], in_=k_acc[:])
+        def empty_banks(c, h, k_acc, v_acc):
+            nc.vector.tensor_copy(
+                out=v_tiles[c][:, h * TILES_PER_HALF : (h + 1) * TILES_PER_HALF, :], in_=v_acc[:]
+            )
+            if c == FIRST:
+                nc.scalar.copy(out=k_first[:, h, :], in_=k_acc[:])
+            if c == LAST - 1:
+                nc.scalar.copy(out=k_middle[:, h, :], in_=k_acc[:])
                 nc.vector.tensor_tensor(
-                    out=k["banksT"][:, 0, :], in0=k["middle"][:], in1=k["first"][:], op=ADD
+                    out=k_sumsT[:, 0, h, :], in0=k_middle[:, h, :], in1=k_first[:, h, :], op=ADD
                 )
-            if c == CHUNKS_PER_BATCH - 1:
+            if c == LAST:
                 nc.vector.tensor_tensor(
-                    out=k["banksT"][:, 2, :], in0=k_acc[:], in1=k["middle"][:], op=ADD
+                    out=k_sumsT[:, 2, h, :], in0=k_acc[:], in1=k_middle[:, h, :], op=ADD
                 )
                 nc.vector.tensor_tensor(
-                    out=k["banksT"][:, 1, :], in0=k_acc[:], in1=k["banksT"][:, 0, :], op=ADD
+                    out=k_sumsT[:, 1, h, :], in0=k_acc[:], in1=k_sumsT[:, 0, h, :], op=ADD
                 )
 
-        def turn_k_back(b):
-            k = k_sums[b]
-            for j in range(3):
+        def turn_k_back(j):
+            for h in range(HALVES):
                 turned = turn_psum.tile([P, BANK], F32, name="turned")
-                for t in range(TILES):
+                for i in range(TILES_PER_HALF):
                     nc.tensor.transpose(
-                        turned[:, t * D_HEAD : (t + 1) * D_HEAD],
-                        k["banksT"][:, j, t * P : (t + 1) * P],
+                        turned[:, i * D_HEAD : (i + 1) * D_HEAD],
+                        k_sumsT[:, j, h, i * P : (i + 1) * P],
                         ident[:],
                     )
-                if j % 2 == 0:
-                    nc.vector.tensor_copy(out=k["banks"][:, j, :], in_=turned[:])
+                if h == 0:
+                    nc.vector.tensor_copy(out=k_sums[:, j, h, :], in_=turned[:])
                 else:
-                    nc.scalar.copy(out=k["banks"][:, j, :], in_=turned[:])
+                    nc.scalar.copy(out=k_sums[:, j, h, :], in_=turned[:])
 
-        for g in range(KV_BUFS):
-            load(g)
+        for c in range(KV_BUFS):
+            load(c)
 
         ident = const.tile([P, P], F32, name="ident")
         make_identity(nc, ident[:])
 
         w_rows = const.tile([P, PACK, 2 * D_HEAD], BF16, name="w_rows")
         nc.scalar.dma_start(
-            out=w_rows[:].rearrange("q (u e) n -> q u (e n)", u=2),
-            in_=Wkv.rearrange("(u q e) n -> q u (e n)", u=2, e=2),
+            out=w_rows[:].rearrange("w (u e) n -> w u (e n)", u=2),
+            in_=Wkv.rearrange("(u w e) n -> w u (e n)", u=2, e=2),
         )
         w_grouped = const.tile([P, 2 * D_HEAD, PACK], BF16, name="w_grouped", align_bytes=64)
-        nc.vector.tensor_copy(out=w_grouped[:], in_=w_rows[:].rearrange("q j n -> q n j"))
+        nc.vector.tensor_copy(out=w_grouped[:], in_=w_rows[:].rearrange("w j n -> w n j"))
         w_codes = const.tile([P, 2 * D_HEAD], U32, name="w_codes", align_bytes=64)
         w_scales = const.tile([P, 2 * D_HEAD], U8, name="w_scales", align_bytes=64)
         nc.vector.quantize_mx(
             out=w_codes[:].bitcast(FP8X4),
             scales=w_scales[:],
-            in_=w_grouped[:].rearrange("q n j -> q (n j)"),
+            in_=w_grouped[:].rearrange("w n j -> w (n j)"),
         )
 
-        for b in range(BATCH):
-            k_sums[b] = {
-                "first": k_pool.tile([P, BANK], F32, name="k_first"),
-                "middle": k_pool.tile([P, BANK], F32, name="k_middle"),
-                "banksT": k_pool.tile([P, 3, BANK], F32, name="k_banksT"),
-                "banks": k_pool.tile([P, 3, BANK], F32, name="k_banks"),
-            }
+        k_first = const.tile([P, HALVES, BANK], F32, name="k_first")
+        k_middle = const.tile([P, HALVES, BANK], F32, name="k_middle")
+        k_sumsT = const.tile([P, K_BANKS, HALVES, BANK], F32, name="k_sumsT")
+        k_sums = const.tile([P, K_BANKS, HALVES, BANK], F32, name="k_sums")
 
-        for r in range(N_ROUNDS + 2):
-            if r >= 2 and (r - 1) % ROUNDS_PER_BATCH == 0:
-                turn_k_back((r - 2) // ROUNDS_PER_BATCH)
-            grouped_tiles = {}
+        for r in range(N_STEPS + 1):
             products = {}
-            if r < N_ROUNDS:
-                for g in range(r * ROUND, (r + 1) * ROUND):
-                    grouped_tiles[g] = transpose_and_regroup(g)
-                    if g + KV_BUFS < N_CHUNKS:
-                        load(g + KV_BUFS)
-            if 1 <= r <= N_ROUNDS:
-                for g in range((r - 1) * ROUND, r * ROUND):
-                    products[g] = multiply(g)
-            for i in range(ROUND):
-                if r < N_ROUNDS:
-                    quantise(r * ROUND + i, grouped_tiles[r * ROUND + i])
-                if 1 <= r <= N_ROUNDS:
-                    empty_banks((r - 1) * ROUND + i, *products[(r - 1) * ROUND + i])
+            if r < N_STEPS:
+                grouped = transpose_and_regroup(r)
+                if r + KV_BUFS < N_STEPS:
+                    load(r + KV_BUFS)
+            else:
+                turn_k_back(0)
+            if r >= 1:
+                v_tiles[r - 1] = v_pool.tile([P, TILES, D_HEAD], F32, name="v_sb")
+                for h in range(HALVES):
+                    products[h] = multiply(r - 1, h)
+            for h in range(HALVES):
+                if r < N_STEPS:
+                    quantise(r, h, grouped)
+                if r >= 1:
+                    empty_banks(r - 1, h, *products[h])
+        turn_k_back(2)
+        turn_k_back(1)
 
-        for b in range(BATCH):
-            for c in range(CHUNKS_PER_BATCH):
+        for c in range(N_STEPS):
+            for b in range(BATCH):
                 rows = v[b, c * CHUNK : (c + 1) * CHUNK, :]
                 nc.sync.dma_start(
-                    out=rows.rearrange("(p t) d -> p t d", t=TILES),
-                    in_=v_tiles[b * CHUNKS_PER_BATCH + c][:],
+                    out=rows.rearrange("(q t) d -> q t d", t=TILES), in_=v_tiles[c][b:P:BATCH, :, :]
                 )
-            nc.sync.dma_start(
-                out=k_ext[b].rearrange("j (p t) d -> p j (t d)", t=TILES),
-                in_=k_sums[b]["banks"][:],
-            )
+        for j in (0, 2, 1):
+            for b in range(BATCH):
+                nc.sync.dma_start(
+                    out=k_ext[b, j].rearrange("(q t) d -> q (t d)", t=TILES),
+                    in_=k_sums[b:P:BATCH, j, :, :].rearrange("q h n -> q (h n)"),
+                )

@@ -14,17 +14,22 @@ P = 128
 PACK = 4
 BATCH, LENGTH, D_MODEL, D_HEAD, CHUNK = 2, 8192, 512, 128, 512
 N_STEPS = LENGTH // CHUNK
+EDGES = 2
 ROWS = BATCH * CHUNK
 TILES = ROWS // P
 BANK = 512
 HALVES = ROWS // BANK
 TILES_PER_HALF = TILES // HALVES
 WORDS = D_MODEL // 2
-K_BANKS = 3
-FIRST, LAST = 0, N_STEPS - 1
+ALL_BUT_LAST, ALL, ALL_BUT_FIRST = 0, 1, 2
 KV_BUFS = N_STEPS // 2
+V_ON_SCALAR_FROM = N_STEPS - 2
 
 FLOPS = 2 * BATCH * LENGTH * D_MODEL * 2 * D_HEAD
+
+
+def chunk_of_step(s):
+    return (0, N_STEPS - 1)[s] if s < EDGES else s - 1
 
 
 def tile_localxlattention_pa_t_kernel(tc, kv, Wkv, k_ext, v):
@@ -44,17 +49,18 @@ def tile_localxlattention_pa_t_kernel(tc, kv, Wkv, k_ext, v):
         v_tiles = {}
         k_open = {}
 
-        def load(c):
+        def chunk_rows(dram, s, b):
+            first = chunk_of_step(s) * CHUNK
+            return dram[b, first : first + CHUNK, :].rearrange("(q t) d -> q (t d)", t=TILES)
+
+        def load(s):
             x = kv_pool.tile([P, TILES * D_MODEL], BF16, name="x")
             for b in range(BATCH):
-                rows = kv[b, c * CHUNK : (c + 1) * CHUNK, :]
-                nc.sync.dma_start(
-                    out=x[b:P:BATCH, :], in_=rows.rearrange("(q t) d -> q (t d)", t=TILES)
-                )
-            kv_tiles[c] = x
+                nc.sync.dma_start(out=x[b:P:BATCH, :], in_=chunk_rows(kv, s, b))
+            kv_tiles[s] = x
 
-        def transpose_and_regroup(c):
-            words = kv_tiles[c][:].bitcast(F32)
+        def transpose_and_regroup(s):
+            words = kv_tiles[s][:].bitcast(F32)
             grouped = mx_pool.tile([P, ROWS * PACK], BF16, name="grouped", align_bytes=64)
             grouped_words = grouped[:].bitcast(F32).rearrange("w (n u) -> w n u", u=2)
             for pair in range(TILES // 2):
@@ -73,11 +79,11 @@ def tile_localxlattention_pa_t_kernel(tc, kv, Wkv, k_ext, v):
                 )
             codes = mx_pool.tile([P, ROWS], U32, name="codes", align_bytes=64)
             scales = mx_pool.tile([P, ROWS], U8, name="scales", align_bytes=64)
-            quantised[c] = (codes, scales)
+            quantised[s] = (codes, scales)
             return grouped
 
-        def quantise(c, h, grouped):
-            codes, scales = quantised[c]
+        def quantise(s, h, grouped):
+            codes, scales = quantised[s]
             cols = slice(h * BANK, (h + 1) * BANK)
             nc.vector.quantize_mx(
                 out=codes[:, cols].bitcast(FP8X4),
@@ -85,11 +91,11 @@ def tile_localxlattention_pa_t_kernel(tc, kv, Wkv, k_ext, v):
                 in_=grouped[:, h * BANK * PACK : (h + 1) * BANK * PACK],
             )
 
-        def multiply(c, h):
-            codes, scales = quantised[c]
+        def multiply(s, h):
+            codes, scales = quantised[s]
             cols = slice(h * BANK, (h + 1) * BANK)
-            start = c in (FIRST, FIRST + 1, LAST)
-            stop = c in (FIRST, LAST - 1, LAST)
+            start = s <= EDGES
+            stop = s < EDGES or s == N_STEPS - 1
             if start:
                 k_open[h] = k_psum.tile([P, BANK], F32, name="k_acc")
             nc.tensor.matmul_mx(
@@ -113,43 +119,27 @@ def tile_localxlattention_pa_t_kernel(tc, kv, Wkv, k_ext, v):
                     start=True,
                     stop=True,
                 )
-            return k_open[h], v_acc
+            return v_acc
 
-        def empty_banks(c, h, k_acc, v_acc):
-            nc.vector.tensor_copy(
-                out=v_tiles[c][:, h * TILES_PER_HALF : (h + 1) * TILES_PER_HALF, :], in_=v_acc[:]
-            )
-            if c == FIRST:
-                nc.scalar.copy(out=k_first[:, h, :], in_=k_acc[:])
-            if c == LAST - 1:
-                nc.scalar.copy(out=k_middle[:, h, :], in_=k_acc[:])
-                nc.vector.tensor_tensor(
-                    out=k_sumsT[:, 0, h, :], in0=k_middle[:, h, :], in1=k_first[:, h, :], op=ADD
-                )
-            if c == LAST:
-                nc.vector.tensor_tensor(
-                    out=k_sumsT[:, 2, h, :], in0=k_acc[:], in1=k_middle[:, h, :], op=ADD
-                )
-                nc.vector.tensor_tensor(
-                    out=k_sumsT[:, 1, h, :], in0=k_acc[:], in1=k_sumsT[:, 0, h, :], op=ADD
-                )
+        def copy_v_out(s, h, v_acc):
+            v_half = v_tiles[s][:, h * TILES_PER_HALF : (h + 1) * TILES_PER_HALF, :]
+            if s >= V_ON_SCALAR_FROM:
+                nc.scalar.copy(out=v_half, in_=v_acc[:])
+            else:
+                nc.vector.tensor_copy(out=v_half, in_=v_acc[:])
 
-        def turn_k_back(j):
-            for h in range(HALVES):
-                turned = turn_psum.tile([P, BANK], F32, name="turned")
-                for i in range(TILES_PER_HALF):
-                    nc.tensor.transpose(
-                        turned[:, i * D_HEAD : (i + 1) * D_HEAD],
-                        k_sumsT[:, j, h, i * P : (i + 1) * P],
-                        ident[:],
-                    )
-                if h == 0:
-                    nc.vector.tensor_copy(out=k_sums[:, j, h, :], in_=turned[:])
-                else:
-                    nc.scalar.copy(out=k_sums[:, j, h, :], in_=turned[:])
+        def turn_k_back(j, h):
+            turned = turn_psum.tile([P, BANK], F32, name="turned")
+            for i in range(TILES_PER_HALF):
+                nc.tensor.transpose(
+                    turned[:, i * D_HEAD : (i + 1) * D_HEAD],
+                    k_sumsT[:, j, h, i * P : (i + 1) * P],
+                    ident[:],
+                )
+            nc.scalar.copy(out=k_sums[:, j, h, :], in_=turned[:])
 
-        for c in range(KV_BUFS):
-            load(c)
+        for s in range(KV_BUFS):
+            load(s)
 
         ident = const.tile([P, P], F32, name="ident")
         make_identity(nc, ident[:])
@@ -169,38 +159,54 @@ def tile_localxlattention_pa_t_kernel(tc, kv, Wkv, k_ext, v):
             in_=w_grouped[:].rearrange("w n j -> w (n j)"),
         )
 
-        k_first = const.tile([P, HALVES, BANK], F32, name="k_first")
-        k_middle = const.tile([P, HALVES, BANK], F32, name="k_middle")
-        k_sumsT = const.tile([P, K_BANKS, HALVES, BANK], F32, name="k_sumsT")
-        k_sums = const.tile([P, K_BANKS, HALVES, BANK], F32, name="k_sums")
+        k_edge = const.tile([P, EDGES, HALVES, BANK], F32, name="k_edge")
+        k_sumsT = const.tile([P, 3, HALVES, BANK], F32, name="k_sumsT")
+        k_sums = const.tile([P, 3, HALVES, BANK], F32, name="k_sums")
 
         for r in range(N_STEPS + 1):
-            products = {}
             if r < N_STEPS:
                 grouped = transpose_and_regroup(r)
                 if r + KV_BUFS < N_STEPS:
                     load(r + KV_BUFS)
-            else:
-                turn_k_back(0)
             if r >= 1:
                 v_tiles[r - 1] = v_pool.tile([P, TILES, D_HEAD], F32, name="v_sb")
-                for h in range(HALVES):
-                    products[h] = multiply(r - 1, h)
+                v_accs = [multiply(r - 1, h) for h in range(HALVES)]
             for h in range(HALVES):
                 if r < N_STEPS:
                     quantise(r, h, grouped)
                 if r >= 1:
-                    empty_banks(r - 1, h, *products[h])
-        turn_k_back(2)
-        turn_k_back(1)
+                    copy_v_out(r - 1, h, v_accs[h])
+            if 1 <= r <= EDGES:
+                for h in range(HALVES):
+                    nc.scalar.copy(out=k_edge[:, r - 1, h, :], in_=k_open[h][:])
 
-        for c in range(N_STEPS):
+        for h in range(HALVES):
+            nc.vector.tensor_tensor(
+                out=k_sumsT[:, ALL_BUT_LAST, h, :], in0=k_open[h][:], in1=k_edge[:, 0, h, :], op=ADD
+            )
+        for h in range(HALVES):
+            nc.vector.tensor_tensor(
+                out=k_sumsT[:, ALL_BUT_FIRST, h, :], in0=k_open[h][:], in1=k_edge[:, 1, h, :], op=ADD
+            )
+        for h in range(HALVES):
+            nc.vector.tensor_tensor(
+                out=k_sumsT[:, ALL, h, :],
+                in0=k_sumsT[:, ALL_BUT_LAST, h, :],
+                in1=k_edge[:, 1, h, :],
+                op=ADD,
+            )
+        banks_as_summed = (ALL_BUT_LAST, ALL_BUT_FIRST, ALL)
+        for j in banks_as_summed:
+            for h in range(HALVES):
+                turn_k_back(j, h)
+
+        for s in range(N_STEPS):
             for b in range(BATCH):
-                rows = v[b, c * CHUNK : (c + 1) * CHUNK, :]
                 nc.sync.dma_start(
-                    out=rows.rearrange("(q t) d -> q t d", t=TILES), in_=v_tiles[c][b:P:BATCH, :, :]
+                    out=chunk_rows(v, s, b),
+                    in_=v_tiles[s][b:P:BATCH, :, :].rearrange("q t d -> q (t d)"),
                 )
-        for j in (0, 2, 1):
+        for j in banks_as_summed:
             for b in range(BATCH):
                 nc.sync.dma_start(
                     out=k_ext[b, j].rearrange("(q t) d -> q (t d)", t=TILES),

from contextlib import ExitStack

import concourse.mybir as mybir
from concourse.masks import make_identity

F32 = mybir.dt.float32
BF16 = mybir.dt.bfloat16
U32 = mybir.dt.uint32
U8 = mybir.dt.uint8
FP8X4 = mybir.dt.float8_e4m3fn_x4
ADD = mybir.AluOpType.add

P = 128
PACK = 4
BATCH, LENGTH, D_MODEL, D_HEAD, CHUNK = 2, 8192, 512, 128, 512
N_STEPS = LENGTH // CHUNK
EDGES = 2
ROWS = BATCH * CHUNK
TILES = ROWS // P
BANK = 512
HALVES = ROWS // BANK
TILES_PER_HALF = TILES // HALVES
WORDS = D_MODEL // 2
ALL_BUT_LAST, ALL, ALL_BUT_FIRST = 0, 1, 2
KV_BUFS = N_STEPS // 2
V_ON_SCALAR_FROM = N_STEPS - 2

FLOPS = 2 * BATCH * LENGTH * D_MODEL * 2 * D_HEAD


def chunk_of_step(s):
    return (0, N_STEPS - 1)[s] if s < EDGES else s - 1


def tile_localxlattention_pa_t_kernel(tc, kv, Wkv, k_ext, v):
    nc = tc.nc
    with ExitStack() as ctx:
        ctx.enter_context(tc.manual_schedule())
        const = ctx.enter_context(tc.tile_pool(name="const", bufs=1))
        kv_pool = ctx.enter_context(tc.tile_pool(name="kv", bufs=KV_BUFS))
        mx_pool = ctx.enter_context(tc.tile_pool(name="mx", bufs=2))
        v_pool = ctx.enter_context(tc.tile_pool(name="v", bufs=N_STEPS))
        turn_psum = ctx.enter_context(tc.psum_pool(name="turn", bufs=4))
        v_psum = ctx.enter_context(tc.psum_pool(name="vp", bufs=HALVES))
        k_psum = ctx.enter_context(tc.psum_pool(name="kp", bufs=HALVES))

        kv_tiles = {}
        quantised = {}
        v_tiles = {}
        k_open = {}

        def chunk_rows(dram, s, b):
            first = chunk_of_step(s) * CHUNK
            return dram[b, first : first + CHUNK, :].rearrange("(q t) d -> q (t d)", t=TILES)

        def load(s):
            x = kv_pool.tile([P, TILES * D_MODEL], BF16, name="x")
            for b in range(BATCH):
                nc.sync.dma_start(out=x[b:P:BATCH, :], in_=chunk_rows(kv, s, b))
            kv_tiles[s] = x

        def transpose_and_regroup(s):
            words = kv_tiles[s][:].bitcast(F32)
            grouped = mx_pool.tile([P, ROWS * PACK], BF16, name="grouped", align_bytes=64)
            grouped_words = grouped[:].bitcast(F32).rearrange("w (n u) -> w n u", u=2)
            for pair in range(TILES // 2):
                turned = turn_psum.tile([P, BANK], F32, name="turned")
                by_u = turned[:].rearrange("w (u n) -> w u n", u=2)
                for i in range(2):
                    t = 2 * pair + i
                    for u in range(2):
                        first = t * WORDS + u * P
                        nc.tensor.transpose(
                            by_u[:, u, i * P : (i + 1) * P], words[:, first : first + P], ident[:]
                        )
                nc.scalar.copy(
                    out=grouped_words[:, 2 * pair * P : 2 * (pair + 1) * P, :],
                    in_=by_u.rearrange("w u n -> w n u"),
                )
            codes = mx_pool.tile([P, ROWS], U32, name="codes", align_bytes=64)
            scales = mx_pool.tile([P, ROWS], U8, name="scales", align_bytes=64)
            quantised[s] = (codes, scales)
            return grouped

        def quantise(s, h, grouped):
            codes, scales = quantised[s]
            cols = slice(h * BANK, (h + 1) * BANK)
            nc.vector.quantize_mx(
                out=codes[:, cols].bitcast(FP8X4),
                scales=scales[:, cols],
                in_=grouped[:, h * BANK * PACK : (h + 1) * BANK * PACK],
            )

        def multiply(s, h):
            codes, scales = quantised[s]
            cols = slice(h * BANK, (h + 1) * BANK)
            start = s <= EDGES
            stop = s < EDGES or s == N_STEPS - 1
            if start:
                k_open[h] = k_psum.tile([P, BANK], F32, name="k_acc")
            nc.tensor.matmul_mx(
                out=k_open[h][:],
                lhsT=w_codes[:, 0:D_HEAD].bitcast(FP8X4),
                lhsT_scale=w_scales[:, 0:D_HEAD],
                rhs=codes[:, cols].bitcast(FP8X4),
                rhs_scale=scales[:, cols],
                start=start,
                stop=stop,
            )
            v_acc = v_psum.tile([P, TILES_PER_HALF, D_HEAD], F32, name="v_acc")
            for i in range(TILES_PER_HALF):
                tile_cols = slice(h * BANK + i * P, h * BANK + (i + 1) * P)
                nc.tensor.matmul_mx(
                    out=v_acc[:, i, :],
                    lhsT=codes[:, tile_cols].bitcast(FP8X4),
                    lhsT_scale=scales[:, tile_cols],
                    rhs=w_codes[:, D_HEAD : 2 * D_HEAD].bitcast(FP8X4),
                    rhs_scale=w_scales[:, D_HEAD : 2 * D_HEAD],
                    start=True,
                    stop=True,
                )
            return v_acc

        def copy_v_out(s, h, v_acc):
            v_half = v_tiles[s][:, h * TILES_PER_HALF : (h + 1) * TILES_PER_HALF, :]
            if s >= V_ON_SCALAR_FROM:
                nc.scalar.copy(out=v_half, in_=v_acc[:])
            else:
                nc.vector.tensor_copy(out=v_half, in_=v_acc[:])

        def turn_k_back(j, h):
            turned = turn_psum.tile([P, BANK], F32, name="turned")
            for i in range(TILES_PER_HALF):
                nc.tensor.transpose(
                    turned[:, i * D_HEAD : (i + 1) * D_HEAD],
                    k_sumsT[:, j, h, i * P : (i + 1) * P],
                    ident[:],
                )
            nc.scalar.copy(out=k_sums[:, j, h, :], in_=turned[:])

        for s in range(KV_BUFS):
            load(s)

        ident = const.tile([P, P], F32, name="ident")
        make_identity(nc, ident[:])

        w_rows = const.tile([P, PACK, 2 * D_HEAD], BF16, name="w_rows")
        nc.scalar.dma_start(
            out=w_rows[:].rearrange("w (u e) n -> w u (e n)", u=2),
            in_=Wkv.rearrange("(u w e) n -> w u (e n)", u=2, e=2),
        )
        w_grouped = const.tile([P, 2 * D_HEAD, PACK], BF16, name="w_grouped", align_bytes=64)
        nc.vector.tensor_copy(out=w_grouped[:], in_=w_rows[:].rearrange("w j n -> w n j"))
        w_codes = const.tile([P, 2 * D_HEAD], U32, name="w_codes", align_bytes=64)
        w_scales = const.tile([P, 2 * D_HEAD], U8, name="w_scales", align_bytes=64)
        nc.vector.quantize_mx(
            out=w_codes[:].bitcast(FP8X4),
            scales=w_scales[:],
            in_=w_grouped[:].rearrange("w n j -> w (n j)"),
        )

        k_edge = const.tile([P, EDGES, HALVES, BANK], F32, name="k_edge")
        k_sumsT = const.tile([P, 3, HALVES, BANK], F32, name="k_sumsT")
        k_sums = const.tile([P, 3, HALVES, BANK], F32, name="k_sums")

        for r in range(N_STEPS + 1):
            if r < N_STEPS:
                grouped = transpose_and_regroup(r)
                if r + KV_BUFS < N_STEPS:
                    load(r + KV_BUFS)
            if r >= 1:
                v_tiles[r - 1] = v_pool.tile([P, TILES, D_HEAD], F32, name="v_sb")
                v_accs = [multiply(r - 1, h) for h in range(HALVES)]
            for h in range(HALVES):
                if r < N_STEPS:
                    quantise(r, h, grouped)
                if r >= 1:
                    copy_v_out(r - 1, h, v_accs[h])
            if 1 <= r <= EDGES:
                for h in range(HALVES):
                    nc.scalar.copy(out=k_edge[:, r - 1, h, :], in_=k_open[h][:])

        for h in range(HALVES):
            nc.vector.tensor_tensor(
                out=k_sumsT[:, ALL_BUT_LAST, h, :], in0=k_open[h][:], in1=k_edge[:, 0, h, :], op=ADD
            )
        for h in range(HALVES):
            nc.vector.tensor_tensor(
                out=k_sumsT[:, ALL_BUT_FIRST, h, :], in0=k_open[h][:], in1=k_edge[:, 1, h, :], op=ADD
            )
        for h in range(HALVES):
            nc.vector.tensor_tensor(
                out=k_sumsT[:, ALL, h, :],
                in0=k_sumsT[:, ALL_BUT_LAST, h, :],
                in1=k_edge[:, 1, h, :],
                op=ADD,
            )
        banks_as_summed = (ALL_BUT_LAST, ALL_BUT_FIRST, ALL)
        for j in banks_as_summed:
            for h in range(HALVES):
                turn_k_back(j, h)

        for s in range(N_STEPS):
            for b in range(BATCH):
                nc.sync.dma_start(
                    out=chunk_rows(v, s, b),
                    in_=v_tiles[s][b:P:BATCH, :, :].rearrange("q t d -> q (t d)"),
                )
        for j in banks_as_summed:
            for b in range(BATCH):
                nc.sync.dma_start(
                    out=k_ext[b, j].rearrange("(q t) d -> q (t d)", t=TILES),
                    in_=k_sums[b:P:BATCH, j, :, :].rearrange("q h n -> q (h n)"),
                )
